import numpy as np
import ml_dtypes


def mxq(x, axis, fmt="e4m3"):
    dtype, down = {"e4m3": (ml_dtypes.float8_e4m3fn, 7), "e5m2": (ml_dtypes.float8_e5m2, 14)}[fmt]
    v = np.moveaxis(np.asarray(x, np.float32).astype(ml_dtypes.bfloat16).astype(np.float64), axis, -1)
    blocks = v.reshape(v.shape[:-1] + (-1, 32))
    amax = np.abs(blocks).max(-1, keepdims=True)
    byte = np.maximum(np.where(amax > 0, np.frexp(amax)[1] - 1 + 127, 0) - down, 1)
    scale = np.exp2(byte - 127.0)
    codes = (blocks / scale).astype(np.float32).astype(dtype).astype(np.float64)
    return np.moveaxis((codes * scale).reshape(v.shape), -1, axis)


WIDE = False


def mx_kscale(k):
    if not WIDE:
        return np.ones(k)
    levels = np.array([10, -10, 5, -5, 0])
    if k % 512:
        return np.exp2(np.random.permutation(np.resize(levels, k // 32))).repeat(32)
    a = np.empty((k // 512, 16))
    for p in range(k // 512):
        a[p, :8] = np.random.permutation(np.resize(levels, 8))
        for g in range(8):
            far = levels[np.abs(levels - a[p, g]) >= 10]
            a[p, g + 8] = far[np.random.randint(len(far))]
    return np.exp2(a.ravel()).repeat(32)


BF16 = ml_dtypes.bfloat16


def bf(x):
    return np.asarray(x, np.float32).astype(BF16)


def f64(x):
    return np.asarray(x).astype(np.float64)


B, IN, H = 512, 1024, 1024


def sigmoid(v):
    return 1.0 / (1.0 + np.exp(-v))


def setup_inputs():
    s, t = mx_kscale(IN), mx_kscale(H)
    wsc = np.sqrt(2.0 / (IN + H))
    usc = 1.0 / np.sqrt(H)
    return {"joint_h": bf(np.random.standard_normal((B, H)) * t),
            "mgn_h": bf(np.random.standard_normal((B, IN)) * s),
            "W_r": bf(np.random.standard_normal((IN, H)) * wsc / s[:, None]),
            "W_h": bf(np.random.standard_normal((IN, H)) * wsc / s[:, None]),
            "U_r": bf(np.random.standard_normal((H, H)) * usc / t[:, None]),
            "U_h": bf(np.random.standard_normal((H, H)) * usc / t[:, None]),
            "b_r": bf(np.random.standard_normal(H) * 0.5),
            "b_h": bf(np.random.standard_normal(H) * 0.5)}


def reference(joint_h, mgn_h, W_r, W_h, U_r, U_h, b_r, b_h):
    h = f64(joint_h)
    xq = mxq(f64(mgn_h), 1, "e4m3")
    r = sigmoid((xq @ mxq(f64(W_r), 0, "e4m3")) + (mxq(h, 1, "e4m3") @ mxq(f64(U_r), 0, "e4m3")) + f64(b_r))
    g = h * r
    return np.tanh((xq @ mxq(f64(W_h), 0, "e4m3")) + (mxq(g, 1, "e4m3") @ mxq(f64(U_h), 0, "e4m3")) + f64(b_h))

@@ -1,0 +1,234 @@
+from contextlib import ExitStack
+
+import concourse.mybir as mybir
+from concourse.masks import make_identity
+
+FLOPS = 4 * 2 * 512 * 1024 * 1024
+
+F32 = mybir.dt.float32
+BF16 = mybir.dt.bfloat16
+I32 = mybir.dt.int32
+U32 = mybir.dt.uint32
+U8 = mybir.dt.uint8
+FP8X4 = mybir.dt.float8_e4m3fn_x4
+ACT = mybir.ActivationFunctionType
+ALU = mybir.AluOpType
+
+P = 128
+PACK = 4
+PASSES = 2
+BATCH = 512
+WIDTH = 1024
+UNIT = 512
+HALF = UNIT // 2
+TILES = UNIT // P
+
+UNITS = [(name, g, half) for name in ("W_r", "U_r", "W_h") for g in range(PASSES) for half in range(2)] + [
+    ("U_h", g, half) for half in range(2) for g in range(PASSES)
+]
+ACTIVATION_OF = {"W_r": "x", "U_r": "h", "W_h": "x", "U_h": "g"}
+STAGE_2 = 8
+
+
+def regrouping_engines(i):
+    if i in (STAGE_2 + 1, STAGE_2 + 2):
+        return ("vector", "vector")
+    if i in (STAGE_2, STAGE_2 + 3, STAGE_2 + 4):
+        return ("scalar", "scalar")
+    return ("vector", "scalar")
+
+
+def tile_joint_gru_pa_kernel(tc, joint_h, mgn_h, W_r, W_h, U_r, U_h, b_r, b_h, out):
+    nc = tc.nc
+    with ExitStack() as ctx:
+        const = ctx.enter_context(tc.tile_pool(name="const", bufs=1))
+        raw = ctx.enter_context(tc.tile_pool(name="raw", bufs=1))
+        keep = ctx.enter_context(tc.tile_pool(name="keep", bufs=1))
+        regrouped = ctx.enter_context(tc.tile_pool(name="regrouped", bufs=6))
+        results = ctx.enter_context(tc.tile_pool(name="results", bufs=8))
+        psum = ctx.enter_context(tc.psum_pool(name="psum", bufs=1))
+        ctx.enter_context(tc.manual_schedule())
+
+        def bank(i, shape, dtype, name):
+            return psum.tile(shape, dtype, name=name, tag="bank%d" % i)
+
+        br_rows = const.tile([P, 4 * P], BF16, name="br_rows")
+        nc.vector.memset(br_rows[:].bitcast(I32), 0)
+        warm = const.tile([P, 8], F32, name="warm")
+        nc.vector.memset(warm[:], 0.0)
+        nc.scalar.activation(out=warm[:, 4:5], in_=warm[:, 0:1], func=ACT.Sigmoid)
+        identity = const.tile([P, P], F32, name="identity")
+        make_identity(nc, identity[:])
+
+        act_raw = {}
+        for name, src in (("x", mgn_h), ("h", joint_h)):
+            act_raw[name] = raw.tile([P, TILES, WIDTH], BF16, name="raw_" + name)
+            rows = src.rearrange("(p a) k -> p a k", a=TILES)
+            for pair in range(2):
+                nc.sync.dma_start(out=act_raw[name][:, 2 * pair : 2 * pair + 2, :], in_=rows[:, 2 * pair : 2 * pair + 2, :])
+        nc.sync.dma_start(out=br_rows[0:2, :], in_=b_r.rearrange("(g n) -> g n", g=2))
+        weight_raw = {}
+        for name, src in (("W_r", W_r), ("U_r", U_r), ("W_h", W_h), ("U_h", U_h)):
+            weight_raw[name] = raw.tile([P, PASSES, PACK, WIDTH], BF16, name="raw_" + name)
+            for g in range(PASSES):
+                nc.sync.dma_start(
+                    out=weight_raw[name][:, g].rearrange("q t n -> q (t n)"),
+                    in_=src[UNIT * g : UNIT * (g + 1), :].rearrange("(q t) n -> q (t n)", t=PACK),
+                )
+        bh_all = const.tile([P, WIDTH], BF16, name="bh_all")
+        nc.sync.dma_start(out=bh_all[:], in_=b_h.partition_broadcast(P))
+
+        words = {}
+        scales = {}
+        for name in ("W_r", "U_r", "W_h", "U_h"):
+            words[name] = keep.tile([P, PASSES, WIDTH], U32, name="words_" + name, align_bytes=64)
+            scales[name] = keep.tile([P, PASSES, WIDTH], U8, name="scales_" + name, align_bytes=64)
+        grouped = {}
+        for name in ("x", "h", "g"):
+            words[name] = keep.tile([P, PASSES, BATCH], U32, name="words_" + name, align_bytes=64)
+            scales[name] = keep.tile([P, PASSES, BATCH], U8, name="scales_" + name, align_bytes=64)
+            grouped[name] = keep.tile([P, PASSES, PACK * BATCH], BF16, name="grouped_" + name, align_bytes=64)
+
+        def quantise_activation(name):
+            nc.vector.quantize_mx(
+                out=words[name][:].rearrange("q g b -> q (g b)").bitcast(FP8X4),
+                scales=scales[name][:].rearrange("q g b -> q (g b)"),
+                in_=grouped[name][:].rearrange("q g n -> q (g n)"),
+            )
+
+        def copy(engine, dst, src):
+            if engine == "vector":
+                nc.vector.tensor_copy(out=dst, in_=src)
+            else:
+                nc.scalar.copy(out=dst, in_=src)
+
+        transposed = {}
+        for first_bank, name in ((0, "x"), (4, "h")):
+            for pair in range(2):
+                for g in range(PASSES):
+                    block = bank(first_bank + 2 * pair + g, [P, 2, 2, P], F32, "transposed")
+                    transposed[(name, pair, g)] = block
+                    for c in range(2):
+                        pairs_of_k = act_raw[name][:, 2 * pair + c, :].bitcast(F32)
+                        for u in range(2):
+                            words_u = slice(2 * P * g + u, 2 * P * (g + 1), 2)
+                            nc.tensor.transpose(block[:, c, u, :], pairs_of_k[:, words_u], identity[:])
+
+        for name in ("x", "h"):
+            for pair in range(2):
+                for g in range(PASSES):
+                    nc.scalar.copy(
+                        out=grouped[name][:, g, :]
+                        .bitcast(F32)[:, UNIT * pair : UNIT * (pair + 1)]
+                        .rearrange("q (c b u) -> q c b u", c=2, b=P, u=2),
+                        in_=transposed[(name, pair, g)][:].rearrange("q c u b -> q c b u"),
+                    )
+        quantise_activation("x")
+
+        br_ps = bank(0, [P, 2, P], F32, "br_ps")
+        for u in range(2):
+            nc.tensor.transpose(br_ps[:, u, :], br_rows[:].bitcast(F32)[:, u : 2 * P : 2], identity[:])
+        br_col = const.tile([P, WIDTH // P], F32, name="br_col")
+        nc.vector.tensor_copy(
+            out=br_col[:].rearrange("q (g u e) -> q u g e", g=PASSES, u=2),
+            in_=br_ps[:, :, 0:PASSES].bitcast(BF16).rearrange("q u (g e) -> q u g e", e=2),
+        )
+
+        unit_tile = {}
+
+        def regroup(i):
+            name, g, half = UNITS[i]
+            unit_tile[i] = regrouped.tile([P, UNIT, PACK], BF16, name="unit", tag="unit", align_bytes=64)
+            for part in (1, 0):
+                src = weight_raw[name][:, g, :, UNIT * half + HALF * part : UNIT * half + HALF * (part + 1)]
+                if i < STAGE_2:
+                    runs = slice(HALF // 4 * part, HALF // 4 * (part + 1))
+                    dst = unit_tile[i][:].rearrange("q (c m) t -> q m t c", c=TILES)[:, runs]
+                    src = src.rearrange("q t (m c) -> q m t c", c=TILES)
+                else:
+                    dst = unit_tile[i][:, HALF * part : HALF * (part + 1), :].rearrange("q (c i) t -> q c t i", i=4)
+                    src = src.rearrange("q t (c i) -> q c t i", i=4)
+                copy(regrouping_engines(i)[part], dst, src)
+
+        def quantise(i):
+            name, g, half = UNITS[i]
+            cols = slice(UNIT * half, UNIT * (half + 1))
+            nc.vector.quantize_mx(
+                out=words[name][:, g, cols].bitcast(FP8X4),
+                scales=scales[name][:, g, cols],
+                in_=unit_tile[i][:].rearrange("q n t -> q (n t)"),
+            )
+
+        sums = {}
+
+        def multiply(i):
+            name, g, half = UNITS[i]
+            act = ACTIVATION_OF[name]
+            opens = name[0] == "W" and g == 0
+            closes = name[0] == "U" and g == PASSES - 1
+            for tile in range(TILES):
+                if i < STAGE_2:
+                    key = ("r", TILES * half + tile)
+                    stationary, s_cols = name, slice(UNIT * half + P * tile, UNIT * half + P * (tile + 1))
+                    moving, m_cols = act, slice(0, BATCH)
+                else:
+                    key = ("out", half, tile)
+                    stationary, s_cols = act, slice(P * tile, P * (tile + 1))
+                    moving, m_cols = name, slice(UNIT * half, UNIT * (half + 1))
+                if opens:
+                    sums[key] = bank(TILES * half + tile, [P, UNIT], F32, "sums")
+                nc.tensor.matmul_mx(
+                    out=sums[key][:],
+                    lhsT=words[stationary][:, g, s_cols].bitcast(FP8X4),
+                    lhsT_scale=scales[stationary][:, g, s_cols],
+                    rhs=words[moving][:, g, m_cols].bitcast(FP8X4),
+                    rhs_scale=scales[moving][:, g, m_cols],
+                    start=opens,
+                    stop=closes,
+                )
+
+        r_runs = [keep.tile([P, BATCH // 4, PACK, 4], F32, name="r_runs%d" % g) for g in range(PASSES)]
+
+        def sigmoid(g):
+            for t in range(PACK):
+                m = PACK * g + t
+                nc.scalar.activation(
+                    out=r_runs[g][:, :, t, :],
+                    in_=sums[("r", m)][:].rearrange("q (c i) -> q c i", i=4),
+                    func=ACT.Sigmoid,
+                    bias=br_col[:, m : m + 1],
+                    scale=1.0,
+                )
+
+        def gate(g):
+            nc.vector.tensor_tensor(
+                out=grouped["g"][:, g, :].rearrange("q (c i t) -> q c t i", i=4, t=PACK),
+                in0=r_runs[g][:],
+                in1=grouped["h"][:, g, :].rearrange("q (c i t) -> q c t i", i=4, t=PACK),
+                op=ALU.mult,
+            )
+
+        for i in range(len(UNITS) + 2):
+            if i < len(UNITS):
+                regroup(i)
+            if i == 1:
+                quantise_activation("h")
+            if 1 <= i <= len(UNITS):
+                quantise(i - 1)
+            if i >= 2:
+                multiply(i - 2)
+            if i in (STAGE_2, STAGE_2 + 1):
+                sigmoid(i - STAGE_2)
+            if i in (STAGE_2 + 2, STAGE_2 + 3):
+                gate(i - STAGE_2 - 2)
+            if i == STAGE_2 + 3:
+                quantise_activation("g")
+
+        out_rows = out.rearrange("(p a) n -> p a n", a=TILES)
+        for j in range(2):
+            cols = slice(UNIT * j, UNIT * (j + 1))
+            for a in range(TILES):
+                result = results.tile([P, UNIT], F32, name="result", tag="result")
+                nc.vector.tensor_tensor(out=result[:], in0=sums[("out", j, a)][:], in1=bh_all[:, cols], op=ALU.add)
+                nc.scalar.activation(out=result[:], in_=result[:], func=ACT.Tanh)
+                nc.sync.dma_start(out=out_rows[:, a, cols], in_=result[:])

@@ -61,20 +61,32 @@ def tile_joint_gru_pa_kernel(tc, joint_h, mgn_h, W_r, W_h, U_r, U_h, b_r, b_h, o
         make_identity(nc, identity[:])
 
         act_raw = {}
-        for name, src in (("x", mgn_h), ("h", joint_h)):
+
+        def load_activation(name, src):
             act_raw[name] = raw.tile([P, TILES, WIDTH], BF16, name="raw_" + name)
             rows = src.rearrange("(p a) k -> p a k", a=TILES)
             for pair in range(2):
                 nc.sync.dma_start(out=act_raw[name][:, 2 * pair : 2 * pair + 2, :], in_=rows[:, 2 * pair : 2 * pair + 2, :])
-        nc.sync.dma_start(out=br_rows[0:2, :], in_=b_r.rearrange("(g n) -> g n", g=2))
+
         weight_raw = {}
-        for name, src in (("W_r", W_r), ("U_r", U_r), ("W_h", W_h), ("U_h", U_h)):
-            weight_raw[name] = raw.tile([P, PASSES, PACK, WIDTH], BF16, name="raw_" + name)
+
+        def load_weight(name, src, g, pieces=1):
+            rows = src[UNIT * g : UNIT * (g + 1), :].rearrange("(q t) n -> q t n", t=PACK)
+            width = WIDTH // pieces
+            for piece in range(pieces):
+                tile = raw.tile([P, PACK, width], BF16, name="raw_%s_%d_%d" % (name, g, piece))
+                nc.sync.dma_start(out=tile[:], in_=rows[:, :, width * piece : width * (piece + 1)])
+                for half in range(2 // pieces):
+                    weight_raw[(name, g, piece + half)] = tile[:, :, UNIT * half : UNIT * (half + 1)]
+
+        nc.scalar.dma_start(out=br_rows[0:2, :], in_=b_r.rearrange("(g n) -> g n", g=2))
+        load_weight("W_r", W_r, 0, 2)
+        load_activation("x", mgn_h)
+        load_weight("W_r", W_r, 1)
+        load_activation("h", joint_h)
+        for name, src in (("U_r", U_r), ("W_h", W_h), ("U_h", U_h)):
             for g in range(PASSES):
-                nc.sync.dma_start(
-                    out=weight_raw[name][:, g].rearrange("q t n -> q (t n)"),
-                    in_=src[UNIT * g : UNIT * (g + 1), :].rearrange("(q t) n -> q (t n)", t=PACK),
-                )
+                load_weight(name, src, g)
         bh_all = const.tile([P, WIDTH], BF16, name="bh_all")
         nc.sync.dma_start(out=bh_all[:], in_=b_h.partition_broadcast(P))
 
@@ -103,7 +115,8 @@ def tile_joint_gru_pa_kernel(tc, joint_h, mgn_h, W_r, W_h, U_r, U_h, b_r, b_h, o
                 nc.scalar.copy(out=dst, in_=src)
 
         transposed = {}
-        for first_bank, name in ((0, "x"), (4, "h")):
+
+        def transpose(name, first_bank):
             for pair in range(2):
                 for g in range(PASSES):
                     block = bank(first_bank + 2 * pair + g, [P, 2, 2, P], F32, "transposed")
@@ -114,7 +127,7 @@ def tile_joint_gru_pa_kernel(tc, joint_h, mgn_h, W_r, W_h, U_r, U_h, b_r, b_h, o
                             words_u = slice(2 * P * g + u, 2 * P * (g + 1), 2)
                             nc.tensor.transpose(block[:, c, u, :], pairs_of_k[:, words_u], identity[:])
 
-        for name in ("x", "h"):
+        def copy_out(name):
             for pair in range(2):
                 for g in range(PASSES):
                     nc.scalar.copy(
@@ -123,16 +136,20 @@ def tile_joint_gru_pa_kernel(tc, joint_h, mgn_h, W_r, W_h, U_r, U_h, b_r, b_h, o
                         .rearrange("q (c b u) -> q c b u", c=2, b=P, u=2),
                         in_=transposed[(name, pair, g)][:].rearrange("q c u b -> q c b u"),
                     )
-        quantise_activation("x")
 
-        br_ps = bank(0, [P, 2, P], F32, "br_ps")
-        for u in range(2):
-            nc.tensor.transpose(br_ps[:, u, :], br_rows[:].bitcast(F32)[:, u : 2 * P : 2], identity[:])
         br_col = const.tile([P, WIDTH // P], F32, name="br_col")
-        nc.vector.tensor_copy(
-            out=br_col[:].rearrange("q (g u e) -> q u g e", g=PASSES, u=2),
-            in_=br_ps[:, :, 0:PASSES].bitcast(BF16).rearrange("q u (g e) -> q u g e", e=2),
-        )
+        br_banks = []
+
+        def transpose_br():
+            br_banks.append(bank(3, [P, 2, P], F32, "br_ps"))
+            for u in range(2):
+                nc.tensor.transpose(br_banks[0][:, u, :], br_rows[:].bitcast(F32)[:, u : 2 * P : 2], identity[:])
+
+        def copy_br():
+            nc.vector.tensor_copy(
+                out=br_col[:].rearrange("q (g u e) -> q u g e", g=PASSES, u=2),
+                in_=br_banks[0][:, :, 0:PASSES].bitcast(BF16).rearrange("q u (g e) -> q u g e", e=2),
+            )
 
         unit_tile = {}
 
@@ -140,7 +157,7 @@ def tile_joint_gru_pa_kernel(tc, joint_h, mgn_h, W_r, W_h, U_r, U_h, b_r, b_h, o
             name, g, half = UNITS[i]
             unit_tile[i] = regrouped.tile([P, UNIT, PACK], BF16, name="unit", tag="unit", align_bytes=64)
             for part in (1, 0):
-                src = weight_raw[name][:, g, :, UNIT * half + HALF * part : UNIT * half + HALF * (part + 1)]
+                src = weight_raw[(name, g, half)][:, :, HALF * part : HALF * (part + 1)]
                 if i < STAGE_2:
                     runs = slice(HALF // 4 * part, HALF // 4 * (part + 1))
                     dst = unit_tile[i][:].rearrange("q (c m) t -> q m t c", c=TILES)[:, runs]
@@ -208,15 +225,33 @@ def tile_joint_gru_pa_kernel(tc, joint_h, mgn_h, W_r, W_h, U_r, U_h, b_r, b_h, o
                 op=ALU.mult,
             )
 
-        for i in range(len(UNITS) + 2):
+        transpose("x", 0)
+        regroup(0)
+        regroup(1)
+        quantise(0)
+        quantise(1)
+        copy_out("x")
+        regroup(2)
+        quantise_activation("x")
+        transpose("h", 4)
+        transpose_br()
+        regroup(3)
+        quantise(2)
+        quantise(3)
+        copy_br()
+        multiply(0)
+        multiply(2)
+        copy_out("h")
+        regroup(4)
+        multiply(1)
+        multiply(3)
+        quantise_activation("h")
+        for i in range(5, len(UNITS) + 1):
             if i < len(UNITS):
                 regroup(i)
-            if i == 1:
-                quantise_activation("h")
-            if 1 <= i <= len(UNITS):
-                quantise(i - 1)
-            if i >= 2:
-                multiply(i - 2)
+            quantise(i - 1)
+            for k in {5: (4,), 6: (), 7: (6, 5), 8: (7,)}.get(i, (i - 1,)):
+                multiply(k)
             if i in (STAGE_2, STAGE_2 + 1):
                 sigmoid(i - STAGE_2)
             if i in (STAGE_2 + 2, STAGE_2 + 3):

@@ -30,12 +30,8 @@ ACTIVATION_OF = {"W_r": "x", "U_r": "h", "W_h": "x", "U_h": "g"}
 STAGE_2 = 8
 
 
-def regrouping_engines(i):
-    if i in (STAGE_2 + 1, STAGE_2 + 2):
-        return ("vector", "vector")
-    if i in (STAGE_2, STAGE_2 + 3, STAGE_2 + 4):
-        return ("scalar", "scalar")
-    return ("vector", "scalar")
+def vector_quarters(i):
+    return {8: 0, 9: 4, 10: 4, 11: 0, 12: 0, 13: 1}.get(i, 2)
 
 
 def tile_joint_gru_pa_kernel(tc, joint_h, mgn_h, W_r, W_h, U_r, U_h, b_r, b_h, out):
@@ -156,16 +152,18 @@ def tile_joint_gru_pa_kernel(tc, joint_h, mgn_h, W_r, W_h, U_r, U_h, b_r, b_h, o
         def regroup(i):
             name, g, half = UNITS[i]
             unit_tile[i] = regrouped.tile([P, UNIT, PACK], BF16, name="unit", tag="unit", align_bytes=64)
-            for part in (1, 0):
-                src = weight_raw[(name, g, half)][:, :, HALF * part : HALF * (part + 1)]
+            split = P // 4 * vector_quarters(i)
+            for engine, runs in (("scalar", slice(split, P)), ("vector", slice(0, split))):
+                if runs.start == runs.stop:
+                    continue
+                src = weight_raw[(name, g, half)][:]
                 if i < STAGE_2:
-                    runs = slice(HALF // 4 * part, HALF // 4 * (part + 1))
-                    dst = unit_tile[i][:].rearrange("q (c m) t -> q m t c", c=TILES)[:, runs]
+                    dst = unit_tile[i][:].rearrange("q (c m) t -> q m t c", c=TILES)
                     src = src.rearrange("q t (m c) -> q m t c", c=TILES)
                 else:
-                    dst = unit_tile[i][:, HALF * part : HALF * (part + 1), :].rearrange("q (c i) t -> q c t i", i=4)
+                    dst = unit_tile[i][:].rearrange("q (c i) t -> q c t i", i=4)
                     src = src.rearrange("q t (c i) -> q c t i", i=4)
-                copy(regrouping_engines(i)[part], dst, src)
+                copy(engine, dst[:, runs], src[:, runs])
 
         def quantise(i):
             name, g, half = UNITS[i]
@@ -250,13 +248,15 @@ def tile_joint_gru_pa_kernel(tc, joint_h, mgn_h, W_r, W_h, U_r, U_h, b_r, b_h, o
             if i < len(UNITS):
                 regroup(i)
             quantise(i - 1)
-            for k in {5: (4,), 6: (), 7: (6, 5), 8: (7,)}.get(i, (i - 1,)):
+            for k in {5: (4,), 6: (), 7: (6, 5)}.get(i, (i - 1,)):
                 multiply(k)
             if i in (STAGE_2, STAGE_2 + 1):
                 sigmoid(i - STAGE_2)
-            if i in (STAGE_2 + 2, STAGE_2 + 3):
-                gate(i - STAGE_2 - 2)
+            if i == STAGE_2 + 2:
+                gate(0)
             if i == STAGE_2 + 3:
+                gate(1)
+            if i == STAGE_2 + 4:
                 quantise_activation("g")
 
         out_rows = out.rearrange("(p a) n -> p a n", a=TILES)

@@ -31,7 +31,7 @@ STAGE_2 = 8
 
 
 def vector_quarters(i):
-    return {8: 0, 9: 4, 10: 4, 11: 0, 12: 0, 13: 1}.get(i, 2)
+    return {8: 0, 9: 4, 10: 4, 11: 0, 12: 0, 15: 0}.get(i, 2)
 
 
 def tile_joint_gru_pa_kernel(tc, joint_h, mgn_h, W_r, W_h, U_r, U_h, b_r, b_h, out):
@@ -66,17 +66,15 @@ def tile_joint_gru_pa_kernel(tc, joint_h, mgn_h, W_r, W_h, U_r, U_h, b_r, b_h, o
 
         weight_raw = {}
 
-        def load_weight(name, src, g, pieces=1):
-            rows = src[UNIT * g : UNIT * (g + 1), :].rearrange("(q t) n -> q t n", t=PACK)
-            width = WIDTH // pieces
-            for piece in range(pieces):
-                tile = raw.tile([P, PACK, width], BF16, name="raw_%s_%d_%d" % (name, g, piece))
-                nc.sync.dma_start(out=tile[:], in_=rows[:, :, width * piece : width * (piece + 1)])
-                for half in range(2 // pieces):
-                    weight_raw[(name, g, piece + half)] = tile[:, :, UNIT * half : UNIT * (half + 1)]
+        def load_weight(name, src, g):
+            tile = raw.tile([P, PACK, WIDTH], BF16, name="raw_%s_%d" % (name, g))
+            rows = src[UNIT * g : UNIT * (g + 1), :]
+            nc.sync.dma_start(out=tile[:].rearrange("q t n -> q (t n)"), in_=rows.rearrange("(q t) n -> q (t n)", t=PACK))
+            for half in range(2):
+                weight_raw[(name, g, half)] = tile[:, :, UNIT * half : UNIT * (half + 1)]
 
         nc.scalar.dma_start(out=br_rows[0:2, :], in_=b_r.rearrange("(g n) -> g n", g=2))
-        load_weight("W_r", W_r, 0, 2)
+        load_weight("W_r", W_r, 0)
         load_activation("x", mgn_h)
         load_weight("W_r", W_r, 1)
         load_activation("h", joint_h)
@@ -223,6 +221,15 @@ def tile_joint_gru_pa_kernel(tc, joint_h, mgn_h, W_r, W_h, U_r, U_h, b_r, b_h, o
                 op=ALU.mult,
             )
 
+        out_rows = out.rearrange("(p a) n -> p a n", a=TILES)
+
+        def finish(j, a):
+            cols = slice(UNIT * j, UNIT * (j + 1))
+            result = results.tile([P, UNIT], F32, name="result", tag="result")
+            nc.vector.tensor_tensor(out=result[:], in0=sums[("out", j, a)][:], in1=bh_all[:, cols], op=ALU.add)
+            nc.scalar.activation(out=result[:], in_=result[:], func=ACT.Tanh)
+            nc.sync.dma_start(out=out_rows[:, a, cols], in_=result[:])
+
         transpose("x", 0)
         regroup(0)
         regroup(1)
@@ -244,9 +251,8 @@ def tile_joint_gru_pa_kernel(tc, joint_h, mgn_h, W_r, W_h, U_r, U_h, b_r, b_h, o
         multiply(1)
         multiply(3)
         quantise_activation("h")
-        for i in range(5, len(UNITS) + 1):
-            if i < len(UNITS):
-                regroup(i)
+        for i in range(5, len(UNITS)):
+            regroup(i)
             quantise(i - 1)
             for k in {5: (4,), 6: (), 7: (6, 5)}.get(i, (i - 1,)):
                 multiply(k)
@@ -258,12 +264,11 @@ def tile_joint_gru_pa_kernel(tc, joint_h, mgn_h, W_r, W_h, U_r, U_h, b_r, b_h, o
                 gate(1)
             if i == STAGE_2 + 4:
                 quantise_activation("g")
-
-        out_rows = out.rearrange("(p a) n -> p a n", a=TILES)
-        for j in range(2):
-            cols = slice(UNIT * j, UNIT * (j + 1))
-            for a in range(TILES):
-                result = results.tile([P, UNIT], F32, name="result", tag="result")
-                nc.vector.tensor_tensor(out=result[:], in0=sums[("out", j, a)][:], in1=bh_all[:, cols], op=ALU.add)
-                nc.scalar.activation(out=result[:], in_=result[:], func=ACT.Tanh)
-                nc.sync.dma_start(out=out_rows[:, a, cols], in_=result[:])
+        finish(0, 0)
+        finish(0, 1)
+        quantise(15)
+        multiply(15)
+        finish(0, 2)
+        finish(0, 3)
+        for a in range(TILES):
+            finish(1, a)

@@ -73,12 +73,14 @@ def tile_joint_gru_pa_kernel(tc, joint_h, mgn_h, W_r, W_h, U_r, U_h, b_r, b_h, o
             for half in range(2):
                 weight_raw[(name, g, half)] = tile[:, :, UNIT * half : UNIT * (half + 1)]
 
-        nc.scalar.dma_start(out=br_rows[0:2, :], in_=b_r.rearrange("(g n) -> g n", g=2))
         load_weight("W_r", W_r, 0)
+        nc.sync.dma_start(out=br_rows[0:2, :], in_=b_r.rearrange("(g n) -> g n", g=2))
         load_activation("x", mgn_h)
         load_weight("W_r", W_r, 1)
+        load_weight("U_r", U_r, 0)
         load_activation("h", joint_h)
-        for name, src in (("U_r", U_r), ("W_h", W_h), ("U_h", U_h)):
+        load_weight("U_r", U_r, 1)
+        for name, src in (("W_h", W_h), ("U_h", U_h)):
             for g in range(PASSES):
                 load_weight(name, src, g)
         bh_all = const.tile([P, WIDTH], BF16, name="bh_all")
@@ -131,11 +133,16 @@ def tile_joint_gru_pa_kernel(tc, joint_h, mgn_h, W_r, W_h, U_r, U_h, b_r, b_h, o
                         in_=transposed[(name, pair, g)][:].rearrange("q c u b -> q c b u"),
                     )
 
+        def keep_warm():
+            idle = bank(6, [P, UNIT], F32, "idle")
+            for k in range(4):
+                nc.tensor.matmul(idle[:], lhsT=act_raw["x"][:, 0, 0:P], rhs=act_raw["x"][:, 0, 0:UNIT], start=True, stop=True)
+
         br_col = const.tile([P, WIDTH // P], F32, name="br_col")
         br_banks = []
 
         def transpose_br():
-            br_banks.append(bank(3, [P, 2, P], F32, "br_ps"))
+            br_banks.append(bank(7, [P, 2, P], F32, "br_ps"))
             for u in range(2):
                 nc.tensor.transpose(br_banks[0][:, u, :], br_rows[:].bitcast(F32)[:, u : 2 * P : 2], identity[:])
 
@@ -231,6 +238,8 @@ def tile_joint_gru_pa_kernel(tc, joint_h, mgn_h, W_r, W_h, U_r, U_h, b_r, b_h, o
             nc.sync.dma_start(out=out_rows[:, a, cols], in_=result[:])
 
         transpose("x", 0)
+        transpose_br()
+        keep_warm()
         regroup(0)
         regroup(1)
         quantise(0)
@@ -238,26 +247,36 @@ def tile_joint_gru_pa_kernel(tc, joint_h, mgn_h, W_r, W_h, U_r, U_h, b_r, b_h, o
         copy_out("x")
         regroup(2)
         quantise_activation("x")
+        copy_br()
+        multiply(0)
         transpose("h", 4)
-        transpose_br()
         regroup(3)
         quantise(2)
         quantise(3)
-        copy_br()
-        multiply(0)
-        multiply(2)
-        copy_out("h")
         regroup(4)
-        multiply(1)
-        multiply(3)
+        regroup(5)
+        quantise(4)
+        copy_out("h")
+        quantise(5)
+        for i in (2, 1, 3):
+            multiply(i)
+        regroup(6)
         quantise_activation("h")
-        for i in range(5, len(UNITS)):
+        regroup(7)
+        quantise(6)
+        multiply(4)
+        multiply(6)
+        quantise(7)
+        multiply(5)
+        multiply(7)
+        regroup(8)
+        sigmoid(0)
+        for i in range(9, len(UNITS)):
             regroup(i)
             quantise(i - 1)
-            for k in {5: (4,), 6: (), 7: (6, 5)}.get(i, (i - 1,)):
-                multiply(k)
-            if i in (STAGE_2, STAGE_2 + 1):
-                sigmoid(i - STAGE_2)
+            multiply(i - 1)
+            if i == STAGE_2 + 1:
+                sigmoid(1)
             if i == STAGE_2 + 2:
                 gate(0)
             if i == STAGE_2 + 3:

@@ -31,7 +31,7 @@ STAGE_2 = 8
 
 
 def vector_quarters(i):
-    return {8: 0, 9: 4, 10: 4, 11: 0, 12: 0, 15: 0}.get(i, 2)
+    return {2: 3, 8: 0, 9: 4, 10: 4, 11: 0, 12: 0, 15: 0}.get(i, 2)
 
 
 def tile_joint_gru_pa_kernel(tc, joint_h, mgn_h, W_r, W_h, U_r, U_h, b_r, b_h, out):

from contextlib import ExitStack

import concourse.mybir as mybir
from concourse.masks import make_identity

FLOPS = 4 * 2 * 512 * 1024 * 1024

F32 = mybir.dt.float32
BF16 = mybir.dt.bfloat16
I32 = mybir.dt.int32
U32 = mybir.dt.uint32
U8 = mybir.dt.uint8
FP8X4 = mybir.dt.float8_e4m3fn_x4
ACT = mybir.ActivationFunctionType
ALU = mybir.AluOpType

P = 128
PACK = 4
PASSES = 2
BATCH = 512
WIDTH = 1024
UNIT = 512
HALF = UNIT // 2
TILES = UNIT // P

UNITS = [(name, g, half) for name in ("W_r", "U_r", "W_h") for g in range(PASSES) for half in range(2)] + [
    ("U_h", g, half) for half in range(2) for g in range(PASSES)
]
ACTIVATION_OF = {"W_r": "x", "U_r": "h", "W_h": "x", "U_h": "g"}
STAGE_2 = 8


def vector_quarters(i):
    return {2: 3, 8: 0, 9: 4, 10: 4, 11: 0, 12: 0, 15: 0}.get(i, 2)


def tile_joint_gru_pa_kernel(tc, joint_h, mgn_h, W_r, W_h, U_r, U_h, b_r, b_h, out):
    nc = tc.nc
    with ExitStack() as ctx:
        const = ctx.enter_context(tc.tile_pool(name="const", bufs=1))
        raw = ctx.enter_context(tc.tile_pool(name="raw", bufs=1))
        keep = ctx.enter_context(tc.tile_pool(name="keep", bufs=1))
        regrouped = ctx.enter_context(tc.tile_pool(name="regrouped", bufs=6))
        results = ctx.enter_context(tc.tile_pool(name="results", bufs=8))
        psum = ctx.enter_context(tc.psum_pool(name="psum", bufs=1))
        ctx.enter_context(tc.manual_schedule())

        def bank(i, shape, dtype, name):
            return psum.tile(shape, dtype, name=name, tag="bank%d" % i)

        br_rows = const.tile([P, 4 * P], BF16, name="br_rows")
        nc.vector.memset(br_rows[:].bitcast(I32), 0)
        warm = const.tile([P, 8], F32, name="warm")
        nc.vector.memset(warm[:], 0.0)
        nc.scalar.activation(out=warm[:, 4:5], in_=warm[:, 0:1], func=ACT.Sigmoid)
        identity = const.tile([P, P], F32, name="identity")
        make_identity(nc, identity[:])

        act_raw = {}

        def load_activation(name, src):
            act_raw[name] = raw.tile([P, TILES, WIDTH], BF16, name="raw_" + name)
            rows = src.rearrange("(p a) k -> p a k", a=TILES)
            for pair in range(2):
                nc.sync.dma_start(out=act_raw[name][:, 2 * pair : 2 * pair + 2, :], in_=rows[:, 2 * pair : 2 * pair + 2, :])

        weight_raw = {}

        def load_weight(name, src, g):
            tile = raw.tile([P, PACK, WIDTH], BF16, name="raw_%s_%d" % (name, g))
            rows = src[UNIT * g : UNIT * (g + 1), :]
            nc.sync.dma_start(out=tile[:].rearrange("q t n -> q (t n)"), in_=rows.rearrange("(q t) n -> q (t n)", t=PACK))
            for half in range(2):
                weight_raw[(name, g, half)] = tile[:, :, UNIT * half : UNIT * (half + 1)]

        load_weight("W_r", W_r, 0)
        nc.sync.dma_start(out=br_rows[0:2, :], in_=b_r.rearrange("(g n) -> g n", g=2))
        load_activation("x", mgn_h)
        load_weight("W_r", W_r, 1)
        load_weight("U_r", U_r, 0)
        load_activation("h", joint_h)
        load_weight("U_r", U_r, 1)
        for name, src in (("W_h", W_h), ("U_h", U_h)):
            for g in range(PASSES):
                load_weight(name, src, g)
        bh_all = const.tile([P, WIDTH], BF16, name="bh_all")
        nc.sync.dma_start(out=bh_all[:], in_=b_h.partition_broadcast(P))

        words = {}
        scales = {}
        for name in ("W_r", "U_r", "W_h", "U_h"):
            words[name] = keep.tile([P, PASSES, WIDTH], U32, name="words_" + name, align_bytes=64)
            scales[name] = keep.tile([P, PASSES, WIDTH], U8, name="scales_" + name, align_bytes=64)
        grouped = {}
        for name in ("x", "h", "g"):
            words[name] = keep.tile([P, PASSES, BATCH], U32, name="words_" + name, align_bytes=64)
            scales[name] = keep.tile([P, PASSES, BATCH], U8, name="scales_" + name, align_bytes=64)
            grouped[name] = keep.tile([P, PASSES, PACK * BATCH], BF16, name="grouped_" + name, align_bytes=64)

        def quantise_activation(name):
            nc.vector.quantize_mx(
                out=words[name][:].rearrange("q g b -> q (g b)").bitcast(FP8X4),
                scales=scales[name][:].rearrange("q g b -> q (g b)"),
                in_=grouped[name][:].rearrange("q g n -> q (g n)"),
            )

        def copy(engine, dst, src):
            if engine == "vector":
                nc.vector.tensor_copy(out=dst, in_=src)
            else:
                nc.scalar.copy(out=dst, in_=src)

        transposed = {}

        def transpose(name, first_bank):
            for pair in range(2):
                for g in range(PASSES):
                    block = bank(first_bank + 2 * pair + g, [P, 2, 2, P], F32, "transposed")
                    transposed[(name, pair, g)] = block
                    for c in range(2):
                        pairs_of_k = act_raw[name][:, 2 * pair + c, :].bitcast(F32)
                        for u in range(2):
                            words_u = slice(2 * P * g + u, 2 * P * (g + 1), 2)
                            nc.tensor.transpose(block[:, c, u, :], pairs_of_k[:, words_u], identity[:])

        def copy_out(name):
            for pair in range(2):
                for g in range(PASSES):
                    nc.scalar.copy(
                        out=grouped[name][:, g, :]
                        .bitcast(F32)[:, UNIT * pair : UNIT * (pair + 1)]
                        .rearrange("q (c b u) -> q c b u", c=2, b=P, u=2),
                        in_=transposed[(name, pair, g)][:].rearrange("q c u b -> q c b u"),
                    )

        def keep_warm():
            idle = bank(6, [P, UNIT], F32, "idle")
            for k in range(4):
                nc.tensor.matmul(idle[:], lhsT=act_raw["x"][:, 0, 0:P], rhs=act_raw["x"][:, 0, 0:UNIT], start=True, stop=True)

        br_col = const.tile([P, WIDTH // P], F32, name="br_col")
        br_banks = []

        def transpose_br():
            br_banks.append(bank(7, [P, 2, P], F32, "br_ps"))
            for u in range(2):
                nc.tensor.transpose(br_banks[0][:, u, :], br_rows[:].bitcast(F32)[:, u : 2 * P : 2], identity[:])

        def copy_br():
            nc.vector.tensor_copy(
                out=br_col[:].rearrange("q (g u e) -> q u g e", g=PASSES, u=2),
                in_=br_banks[0][:, :, 0:PASSES].bitcast(BF16).rearrange("q u (g e) -> q u g e", e=2),
            )

        unit_tile = {}

        def regroup(i):
            name, g, half = UNITS[i]
            unit_tile[i] = regrouped.tile([P, UNIT, PACK], BF16, name="unit", tag="unit", align_bytes=64)
            split = P // 4 * vector_quarters(i)
            for engine, runs in (("scalar", slice(split, P)), ("vector", slice(0, split))):
                if runs.start == runs.stop:
                    continue
                src = weight_raw[(name, g, half)][:]
                if i < STAGE_2:
                    dst = unit_tile[i][:].rearrange("q (c m) t -> q m t c", c=TILES)
                    src = src.rearrange("q t (m c) -> q m t c", c=TILES)
                else:
                    dst = unit_tile[i][:].rearrange("q (c i) t -> q c t i", i=4)
                    src = src.rearrange("q t (c i) -> q c t i", i=4)
                copy(engine, dst[:, runs], src[:, runs])

        def quantise(i):
            name, g, half = UNITS[i]
            cols = slice(UNIT * half, UNIT * (half + 1))
            nc.vector.quantize_mx(
                out=words[name][:, g, cols].bitcast(FP8X4),
                scales=scales[name][:, g, cols],
                in_=unit_tile[i][:].rearrange("q n t -> q (n t)"),
            )

        sums = {}

        def multiply(i):
            name, g, half = UNITS[i]
            act = ACTIVATION_OF[name]
            opens = name[0] == "W" and g == 0
            closes = name[0] == "U" and g == PASSES - 1
            for tile in range(TILES):
                if i < STAGE_2:
                    key = ("r", TILES * half + tile)
                    stationary, s_cols = name, slice(UNIT * half + P * tile, UNIT * half + P * (tile + 1))
                    moving, m_cols = act, slice(0, BATCH)
                else:
                    key = ("out", half, tile)
                    stationary, s_cols = act, slice(P * tile, P * (tile + 1))
                    moving, m_cols = name, slice(UNIT * half, UNIT * (half + 1))
                if opens:
                    sums[key] = bank(TILES * half + tile, [P, UNIT], F32, "sums")
                nc.tensor.matmul_mx(
                    out=sums[key][:],
                    lhsT=words[stationary][:, g, s_cols].bitcast(FP8X4),
                    lhsT_scale=scales[stationary][:, g, s_cols],
                    rhs=words[moving][:, g, m_cols].bitcast(FP8X4),
                    rhs_scale=scales[moving][:, g, m_cols],
                    start=opens,
                    stop=closes,
                )

        r_runs = [keep.tile([P, BATCH // 4, PACK, 4], F32, name="r_runs%d" % g) for g in range(PASSES)]

        def sigmoid(g):
            for t in range(PACK):
                m = PACK * g + t
                nc.scalar.activation(
                    out=r_runs[g][:, :, t, :],
                    in_=sums[("r", m)][:].rearrange("q (c i) -> q c i", i=4),
                    func=ACT.Sigmoid,
                    bias=br_col[:, m : m + 1],
                    scale=1.0,
                )

        def gate(g):
            nc.vector.tensor_tensor(
                out=grouped["g"][:, g, :].rearrange("q (c i t) -> q c t i", i=4, t=PACK),
                in0=r_runs[g][:],
                in1=grouped["h"][:, g, :].rearrange("q (c i t) -> q c t i", i=4, t=PACK),
                op=ALU.mult,
            )

        out_rows = out.rearrange("(p a) n -> p a n", a=TILES)

        def finish(j, a):
            cols = slice(UNIT * j, UNIT * (j + 1))
            result = results.tile([P, UNIT], F32, name="result", tag="result")
            nc.vector.tensor_tensor(out=result[:], in0=sums[("out", j, a)][:], in1=bh_all[:, cols], op=ALU.add)
            nc.scalar.activation(out=result[:], in_=result[:], func=ACT.Tanh)
            nc.sync.dma_start(out=out_rows[:, a, cols], in_=result[:])

        transpose("x", 0)
        transpose_br()
        keep_warm()
        regroup(0)
        regroup(1)
        quantise(0)
        quantise(1)
        copy_out("x")
        regroup(2)
        quantise_activation("x")
        copy_br()
        multiply(0)
        transpose("h", 4)
        regroup(3)
        quantise(2)
        quantise(3)
        regroup(4)
        regroup(5)
        quantise(4)
        copy_out("h")
        quantise(5)
        for i in (2, 1, 3):
            multiply(i)
        regroup(6)
        quantise_activation("h")
        regroup(7)
        quantise(6)
        multiply(4)
        multiply(6)
        quantise(7)
        multiply(5)
        multiply(7)
        regroup(8)
        sigmoid(0)
        for i in range(9, len(UNITS)):
            regroup(i)
            quantise(i - 1)
            multiply(i - 1)
            if i == STAGE_2 + 1:
                sigmoid(1)
            if i == STAGE_2 + 2:
                gate(0)
            if i == STAGE_2 + 3:
                gate(1)
            if i == STAGE_2 + 4:
                quantise_activation("g")
        finish(0, 0)
        finish(0, 1)
        quantise(15)
        multiply(15)
        finish(0, 2)
        finish(0, 3)
        for a in range(TILES):
            finish(1, a)
